import numpy as np
import ml_dtypes


def mxq(x, axis, fmt="e4m3"):
    dtype, down = {"e4m3": (ml_dtypes.float8_e4m3fn, 7), "e5m2": (ml_dtypes.float8_e5m2, 14)}[fmt]
    v = np.moveaxis(np.asarray(x, np.float32).astype(ml_dtypes.bfloat16).astype(np.float64), axis, -1)
    blocks = v.reshape(v.shape[:-1] + (-1, 32))
    amax = np.abs(blocks).max(-1, keepdims=True)
    byte = np.maximum(np.where(amax > 0, np.frexp(amax)[1] - 1 + 127, 0) - down, 1)
    scale = np.exp2(byte - 127.0)
    codes = (blocks / scale).astype(np.float32).astype(dtype).astype(np.float64)
    return np.moveaxis((codes * scale).reshape(v.shape), -1, axis)


WIDE = False


def mx_kscale(k):
    if not WIDE:
        return np.ones(k)
    levels = np.array([10, -10, 5, -5, 0])
    a = np.random.permutation(np.resize(levels, k // 512 * 4)).reshape(k // 512, 4)
    idx = np.arange(k)
    return np.exp2(a[idx // 512, idx % 128 // 32])


BF16 = ml_dtypes.bfloat16


def bf(x):
    return np.asarray(x, np.float32).astype(BF16)


def f64(x):
    return np.asarray(x).astype(np.float64)


B, C, H, W, K, O = 1, 128, 32, 32, 2, 512
P = C * K * K
PAD = 1
G = 32


def im2col(a):
    a_pad = np.pad(a, ((0, 0), (0, 0), (PAD, PAD), (PAD, PAD)), mode="reflect")
    cols = np.stack([a_pad[:, :, kh:kh + H, kw:kw + W] for kh in range(K) for kw in range(K)], axis=2)
    cols = cols.reshape(B, P, H * W)
    return np.swapaxes(cols, 1, 2)


def setup_inputs():
    u = np.unique(mx_kscale(P))
    t = u[np.arange(C // G) % len(u)]
    sc = np.repeat(t, G).reshape(1, C, 1, 1)
    sp = np.repeat(t, G * K * K).reshape(P, 1)
    lam = 1.0 if len(u) == 1 else 0.0
    g = 2.0 ** np.round(0.5 * np.log2(np.mean(t ** 2)))
    amp = 0.5 + 1.5 * np.random.random_sample((B, 1, H, W))
    off = 0.6 + 0.4 * np.random.standard_normal((B, 1, H, W))
    bound = np.sqrt(6.0 / P)
    z = np.random.standard_normal((B, C, H, W))
    z[:, 1::2] = lam * z[:, 1::2] - (1.0 - lam) * z[:, 0::2]
    return {"a": bf((z * amp + off * lam) * sc),
            "conv_kernel": bf(np.random.uniform(-bound, bound, (P, O)) * g / sp)}


def reference(a, conv_kernel):
    patches = im2col(f64(a))
    mean = np.mean(patches, axis=-1, keepdims=True)
    std = np.std(patches, axis=-1, keepdims=True, ddof=1)
    normed = (patches - mean) / std
    out = mxq(normed, 2, "e4m3") @ mxq(f64(conv_kernel), 0, "e4m3")
    return np.swapaxes(out, 1, 2).reshape(B, O, H, W)

@@ -1,0 +1,189 @@
+from contextlib import ExitStack
+
+import concourse.mybir as mybir
+from concourse.masks import make_identity
+
+F32 = mybir.dt.float32
+BF16 = mybir.dt.bfloat16
+U32 = mybir.dt.uint32
+U8 = mybir.dt.uint8
+FP8X4 = mybir.dt.float8_e4m3fn_x4
+ACT = mybir.ActivationFunctionType
+ALU = mybir.AluOpType
+
+P = 128
+SIDE = 32
+TAPS = 4
+PATCH = P * TAPS
+OUT_CH = 512
+PIXELS = SIDE * SIDE
+ROW_WORDS = SIDE // 2
+ROUND_ROWS = P // ROW_WORDS
+ROUNDS = SIDE // ROUND_ROWS
+GROUPS = 2 * ROUNDS
+ROUND_PIXELS = ROUND_ROWS * SIDE
+PADDED = (SIDE + 1) * SIDE
+BANK = 512
+GROUP_WORDS = 2 * P
+PATCH_BANKS = 4
+
+FLOPS = 2 * PIXELS * PATCH * OUT_CH
+
+
+def tile_norm_conv_s_kernel(tc, a, conv_kernel, out):
+    nc = tc.nc
+    a_flat = a.rearrange("b c h w -> (b c) (h w)")
+    out_view = out.rearrange("b (t p) h w -> p (b t) (h w)", p=P)
+
+    with ExitStack() as ctx:
+        keep = ctx.enter_context(tc.tile_pool(name="keep", bufs=1))
+        small = ctx.enter_context(tc.tile_pool(name="small", bufs=PATCH_BANKS))
+        work = ctx.enter_context(tc.tile_pool(name="work", bufs=2))
+        results = ctx.enter_context(tc.tile_pool(name="results", bufs=4))
+        psum_patch = ctx.enter_context(tc.psum_pool(name="psum_patch", bufs=PATCH_BANKS))
+        psum_back = ctx.enter_context(tc.psum_pool(name="psum_back", bufs=2))
+        psum_out = ctx.enter_context(tc.psum_pool(name="psum_out", bufs=2))
+        ctx.enter_context(tc.manual_schedule())
+
+        image = keep.tile([P, PADDED], BF16)
+        shifted = keep.tile([P, PADDED], BF16)
+        w_rows = keep.tile([P, TAPS, OUT_CH], BF16)
+        nc.sync.dma_start(out=image[:, SIDE:PADDED], in_=a_flat)
+        nc.sync.dma_start(out=shifted[:, SIDE + 1 : PADDED], in_=a_flat[:, 0 : PIXELS - 1])
+        nc.sync.dma_start(out=w_rows[:], in_=conv_kernel.rearrange("(c t) o -> c t o", t=TAPS))
+
+        one = keep.tile([P, 1], F32)
+        root_of_one = keep.tile([P, 1], F32)
+        nc.vector.memset(one[:], 1.0)
+        nc.scalar.activation(out=root_of_one[:], in_=one[:], func=ACT.Sqrt)
+        minus_share = keep.tile([P, 1], BF16)
+        nc.vector.memset(minus_share[:], -1.0 / PATCH)
+
+        identity = keep.tile([P, P], F32)
+        make_identity(nc, identity[:])
+
+        image_rows = image[:].rearrange("c (r w) -> c r w", w=SIDE)
+        shifted_rows = shifted[:].rearrange("c (r w) -> c r w", w=SIDE)
+        nc.vector.tensor_copy(out=image_rows[:, 0, :], in_=image_rows[:, 2, :])
+        nc.vector.tensor_copy(out=shifted_rows[:, 1:, 0:1], in_=image_rows[:, 1:, 1:2])
+        nc.vector.tensor_copy(out=shifted_rows[:, 0, :], in_=shifted_rows[:, 2, :])
+
+        w_grouped = keep.tile([P, OUT_CH, TAPS], BF16, align_bytes=64)
+        w_codes = keep.tile([P, OUT_CH], U32, align_bytes=64)
+        w_scales = keep.tile([P, OUT_CH], U8, align_bytes=64)
+        nc.gpsimd.tensor_scalar(
+            out=w_grouped[:],
+            in0=w_rows[:].rearrange("c t o -> c o t"),
+            scalar1=1.0,
+            scalar2=0.0,
+            op0=ALU.mult,
+            op1=ALU.add,
+        )
+
+        source_of_parity = (shifted, image)
+        patch_of_group = {}
+        std_of_group = {}
+        normed_of_round = {}
+        grouped_of_round = {}
+
+        def pixels_onto_partitions(g):
+            r, parity = divmod(g, 2)
+            source = source_of_parity[parity]
+            words = source[:].bitcast(F32)
+            pairs = source[:].rearrange("c (x kw) -> c x kw", kw=2)
+            patch = psum_patch.tile([P, BANK], F32, name="patch")
+            for kh in range(2):
+                first = (ROUND_ROWS * r + kh) * ROW_WORDS
+                nc.tensor.transpose(patch[:, P * kh : P * (kh + 1)], words[:, first : first + P], identity[:])
+            for tap in range(TAPS):
+                kh, kw = divmod(tap, 2)
+                first = (ROUND_ROWS * r + kh) * ROW_WORDS
+                nc.tensor.matmul(
+                    out=patch[:, GROUP_WORDS : GROUP_WORDS + 1],
+                    lhsT=pairs[:, first : first + P, kw],
+                    rhs=minus_share[:],
+                    start=(tap == 0),
+                    stop=(tap == TAPS - 1),
+                )
+            patch_of_group[g] = patch
+
+        def spread(g):
+            values = patch_of_group[g][:].bitcast(BF16)[:, 0:PATCH]
+            stats = small.tile([P, 6], F32, name="stats")
+            mean_var = small.tile([P, 2], F32, name="mean_var")
+            std = small.tile([P, 1], F32, name="std")
+            nc.vector.bn_stats(out=stats[:], in_=values)
+            nc.vector.bn_aggr(out=mean_var[:], in_=stats[:])
+            nc.scalar.activation(out=std[:], in_=mean_var[:, 1:2], func=ACT.Sqrt, scale=PATCH / (PATCH - 1.0))
+            std_of_group[g] = std
+
+        def normalise(g):
+            r, parity = divmod(g, 2)
+            if parity == 0:
+                normed_of_round[r] = work.tile([P, 2 * PATCH], BF16, name="normed")
+            patch = patch_of_group[g]
+            inv_std = small.tile([P, 1], F32, name="inv_std")
+            nc.vector.reciprocal(out=inv_std[:], in_=std_of_group[g][:])
+            nc.vector.tensor_scalar(
+                out=normed_of_round[r][:, PATCH * parity : PATCH * (parity + 1)],
+                in0=patch[:].bitcast(BF16)[:, 0:PATCH],
+                scalar1=patch[:, GROUP_WORDS : GROUP_WORDS + 1],
+                scalar2=inv_std[:],
+                op0=ALU.add,
+                op1=ALU.mult,
+            )
+
+        def channels_onto_partitions(r):
+            normed_words = normed_of_round[r][:].bitcast(F32)
+            back = psum_back.tile([P, BANK], F32, name="back")
+            for slot in range(4):
+                cols = slice(P * slot, P * (slot + 1))
+                nc.tensor.transpose(back[:, cols], normed_words[:, cols], identity[:])
+            grouped = work.tile([P, ROUND_PIXELS * TAPS], BF16, name="grouped", align_bytes=64)
+            nc.scalar.copy(
+                out=grouped[:].bitcast(F32).rearrange("c (q s k) -> c q s k", s=2, k=2),
+                in_=back[:].rearrange("c (s k q) -> c q s k", s=2, k=2),
+            )
+            grouped_of_round[r] = grouped
+
+        def multiply(r):
+            x_codes = work.tile([P, ROUND_PIXELS], U32, name="x_codes", align_bytes=64)
+            x_scales = work.tile([P, ROUND_PIXELS], U8, name="x_scales", align_bytes=64)
+            nc.vector.quantize_mx(out=x_codes[:].bitcast(FP8X4), scales=x_scales[:], in_=grouped_of_round[r][:])
+            pixels = slice(ROUND_PIXELS * r, ROUND_PIXELS * (r + 1))
+            for pair in range(2):
+                acc = psum_out.tile([P, 2, ROUND_PIXELS], F32, name="acc")
+                for half in range(2):
+                    o_cols = slice(P * (2 * pair + half), P * (2 * pair + half + 1))
+                    nc.tensor.matmul_mx(
+                        out=acc[:, half, :],
+                        lhsT=w_codes[:, o_cols].bitcast(FP8X4),
+                        lhsT_scale=w_scales[:, o_cols],
+                        rhs=x_codes[:].bitcast(FP8X4),
+                        rhs_scale=x_scales[:],
+                        start=True,
+                        stop=True,
+                    )
+                result = results.tile([P, 2, ROUND_PIXELS], F32, name="result")
+                nc.scalar.copy(out=result[:], in_=acc[:])
+                nc.sync.dma_start(out=out_view[:, 2 * pair : 2 * pair + 2, pixels], in_=result[:])
+
+        for g in range(PATCH_BANKS):
+            pixels_onto_partitions(g)
+        for g in range(GROUPS + 2):
+            if g < GROUPS:
+                spread(g)
+            if 1 <= g <= GROUPS:
+                normalise(g - 1)
+                if g % 2 == 0:
+                    channels_onto_partitions(g // 2 - 1)
+                if g - 1 + PATCH_BANKS < GROUPS:
+                    pixels_onto_partitions(g - 1 + PATCH_BANKS)
+            if g == 3:
+                nc.vector.quantize_mx(
+                    out=w_codes[:].bitcast(FP8X4),
+                    scales=w_scales[:],
+                    in_=w_grouped[:].rearrange("c o t -> c (o t)"),
+                )
+            if g >= 3 and g % 2 == 1:
+                multiply((g - 3) // 2)

@@ -26,6 +26,7 @@ PADDED = (SIDE + 1) * SIDE
 BANK = 512
 GROUP_WORDS = 2 * P
 PATCH_BANKS = 4
+LAG = 2
 
 FLOPS = 2 * PIXELS * PATCH * OUT_CH
 
@@ -85,9 +86,10 @@ def tile_norm_conv_s_kernel(tc, a, conv_kernel, out):
         std_of_group = {}
         normed_of_round = {}
         grouped_of_round = {}
+        products_of_round = {}
 
         def pixels_onto_partitions(g):
-            r, parity = divmod(g, 2)
+            r, parity = g // 2, (g + 1) % 2
             source = source_of_parity[parity]
             words = source[:].bitcast(F32)
             pairs = source[:].rearrange("c (x kw) -> c x kw", kw=2)
@@ -118,8 +120,8 @@ def tile_norm_conv_s_kernel(tc, a, conv_kernel, out):
             std_of_group[g] = std
 
         def normalise(g):
-            r, parity = divmod(g, 2)
-            if parity == 0:
+            r, parity = g // 2, (g + 1) % 2
+            if g % 2 == 0:
                 normed_of_round[r] = work.tile([P, 2 * PATCH], BF16, name="normed")
             patch = patch_of_group[g]
             inv_std = small.tile([P, 1], F32, name="inv_std")
@@ -150,7 +152,6 @@ def tile_norm_conv_s_kernel(tc, a, conv_kernel, out):
             x_codes = work.tile([P, ROUND_PIXELS], U32, name="x_codes", align_bytes=64)
             x_scales = work.tile([P, ROUND_PIXELS], U8, name="x_scales", align_bytes=64)
             nc.vector.quantize_mx(out=x_codes[:].bitcast(FP8X4), scales=x_scales[:], in_=grouped_of_round[r][:])
-            pixels = slice(ROUND_PIXELS * r, ROUND_PIXELS * (r + 1))
             for pair in range(2):
                 acc = psum_out.tile([P, 2, ROUND_PIXELS], F32, name="acc")
                 for half in range(2):
@@ -164,26 +165,35 @@ def tile_norm_conv_s_kernel(tc, a, conv_kernel, out):
                         start=True,
                         stop=True,
                     )
+                products_of_round[r, pair] = acc
+
+        def store(r):
+            pixels = slice(ROUND_PIXELS * r, ROUND_PIXELS * (r + 1))
+            for pair in range(2):
                 result = results.tile([P, 2, ROUND_PIXELS], F32, name="result")
-                nc.scalar.copy(out=result[:], in_=acc[:])
+                nc.scalar.copy(out=result[:], in_=products_of_round[r, pair][:])
                 nc.sync.dma_start(out=out_view[:, 2 * pair : 2 * pair + 2, pixels], in_=result[:])
 
         for g in range(PATCH_BANKS):
             pixels_onto_partitions(g)
-        for g in range(GROUPS + 2):
-            if g < GROUPS:
-                spread(g)
-            if 1 <= g <= GROUPS:
-                normalise(g - 1)
-                if g % 2 == 0:
-                    channels_onto_partitions(g // 2 - 1)
-                if g - 1 + PATCH_BANKS < GROUPS:
-                    pixels_onto_partitions(g - 1 + PATCH_BANKS)
-            if g == 3:
+        for step in range(GROUPS + 2 * LAG + 1):
+            if step < GROUPS:
+                spread(step)
+            measured = step - LAG
+            if 0 <= measured < GROUPS:
+                normalise(measured)
+                if measured % 2 == 1:
+                    channels_onto_partitions(measured // 2)
+                if measured + PATCH_BANKS < GROUPS:
+                    pixels_onto_partitions(measured + PATCH_BANKS)
+            if step == 2 * LAG:
                 nc.vector.quantize_mx(
                     out=w_codes[:].bitcast(FP8X4),
                     scales=w_scales[:],
                     in_=w_grouped[:].rearrange("c o t -> c (o t)"),
                 )
-            if g >= 3 and g % 2 == 1:
-                multiply((g - 3) // 2)
+            turned = step - 2 * LAG
+            if 0 <= turned < GROUPS and turned % 2 == 1:
+                multiply(turned // 2)
+            if 0 <= turned - 1 < GROUPS and (turned - 1) % 2 == 1:
+                store((turned - 1) // 2)

@@ -83,7 +83,9 @@ def tile_norm_conv_s_kernel(tc, a, conv_kernel, out):
 
         source_of_parity = (shifted, image)
         patch_of_group = {}
+        stats_of_group = {}
         std_of_group = {}
+        inv_std_of_group = {}
         normed_of_round = {}
         grouped_of_round = {}
         products_of_round = {}
@@ -109,23 +111,29 @@ def tile_norm_conv_s_kernel(tc, a, conv_kernel, out):
                 )
             patch_of_group[g] = patch
 
-        def spread(g):
-            values = patch_of_group[g][:].bitcast(BF16)[:, 0:PATCH]
+        def measure(g):
             stats = small.tile([P, 6], F32, name="stats")
+            nc.vector.bn_stats(out=stats[:], in_=patch_of_group[g][:].bitcast(BF16)[:, 0:PATCH])
+            stats_of_group[g] = stats
+
+        def spread(g):
             mean_var = small.tile([P, 2], F32, name="mean_var")
             std = small.tile([P, 1], F32, name="std")
-            nc.vector.bn_stats(out=stats[:], in_=values)
-            nc.vector.bn_aggr(out=mean_var[:], in_=stats[:])
+            nc.vector.bn_aggr(out=mean_var[:], in_=stats_of_group[g][:])
             nc.scalar.activation(out=std[:], in_=mean_var[:, 1:2], func=ACT.Sqrt, scale=PATCH / (PATCH - 1.0))
             std_of_group[g] = std
+
+        def invert(g):
+            inv_std = small.tile([P, 1], F32, name="inv_std")
+            nc.vector.reciprocal(out=inv_std[:], in_=std_of_group[g][:])
+            inv_std_of_group[g] = inv_std
 
         def normalise(g):
             r, parity = g // 2, (g + 1) % 2
             if g % 2 == 0:
                 normed_of_round[r] = work.tile([P, 2 * PATCH], BF16, name="normed")
             patch = patch_of_group[g]
-            inv_std = small.tile([P, 1], F32, name="inv_std")
-            nc.vector.reciprocal(out=inv_std[:], in_=std_of_group[g][:])
+            inv_std = inv_std_of_group[g]
             nc.vector.tensor_scalar(
                 out=normed_of_round[r][:, PATCH * parity : PATCH * (parity + 1)],
                 in0=patch[:].bitcast(BF16)[:, 0:PATCH],
@@ -178,10 +186,15 @@ def tile_norm_conv_s_kernel(tc, a, conv_kernel, out):
             pixels_onto_partitions(g)
         for step in range(GROUPS + 2 * LAG + 1):
             if step < GROUPS:
-                spread(step)
+                measure(step)
             measured = step - LAG
             if 0 <= measured < GROUPS:
                 normalise(measured)
+            if step < GROUPS:
+                spread(step)
+            if 0 <= step - 1 < GROUPS:
+                invert(step - 1)
+            if 0 <= measured < GROUPS:
                 if measured % 2 == 1:
                     channels_onto_partitions(measured // 2)
                 if measured + PATCH_BANKS < GROUPS:

@@ -25,7 +25,7 @@ ROUND_PIXELS = ROUND_ROWS * SIDE
 PADDED = (SIDE + 1) * SIDE
 BANK = 512
 GROUP_WORDS = 2 * P
-PATCH_BANKS = 4
+PATCH_BANKS = 5
 LAG = 2
 
 FLOPS = 2 * PIXELS * PATCH * OUT_CH
@@ -42,7 +42,7 @@ def tile_norm_conv_s_kernel(tc, a, conv_kernel, out):
         work = ctx.enter_context(tc.tile_pool(name="work", bufs=2))
         results = ctx.enter_context(tc.tile_pool(name="results", bufs=4))
         psum_patch = ctx.enter_context(tc.psum_pool(name="psum_patch", bufs=PATCH_BANKS))
-        psum_back = ctx.enter_context(tc.psum_pool(name="psum_back", bufs=2))
+        psum_back = ctx.enter_context(tc.psum_pool(name="psum_back", bufs=1))
         psum_out = ctx.enter_context(tc.psum_pool(name="psum_out", bufs=2))
         ctx.enter_context(tc.manual_schedule())
 
@@ -56,7 +56,7 @@ def tile_norm_conv_s_kernel(tc, a, conv_kernel, out):
         one = keep.tile([P, 1], F32)
         root_of_one = keep.tile([P, 1], F32)
         nc.vector.memset(one[:], 1.0)
-        nc.scalar.activation(out=root_of_one[:], in_=one[:], func=ACT.Sqrt)
+        nc.scalar.activation(out=root_of_one[:], in_=one[:], func=ACT.Abs_reciprocal_sqrt)
         minus_share = keep.tile([P, 1], BF16)
         nc.vector.memset(minus_share[:], -1.0 / PATCH)
 
@@ -84,7 +84,6 @@ def tile_norm_conv_s_kernel(tc, a, conv_kernel, out):
         source_of_parity = (shifted, image)
         patch_of_group = {}
         stats_of_group = {}
-        std_of_group = {}
         inv_std_of_group = {}
         normed_of_round = {}
         grouped_of_round = {}
@@ -118,14 +117,11 @@ def tile_norm_conv_s_kernel(tc, a, conv_kernel, out):
 
         def spread(g):
             mean_var = small.tile([P, 2], F32, name="mean_var")
-            std = small.tile([P, 1], F32, name="std")
-            nc.vector.bn_aggr(out=mean_var[:], in_=stats_of_group[g][:])
-            nc.scalar.activation(out=std[:], in_=mean_var[:, 1:2], func=ACT.Sqrt, scale=PATCH / (PATCH - 1.0))
-            std_of_group[g] = std
-
-        def invert(g):
             inv_std = small.tile([P, 1], F32, name="inv_std")
-            nc.vector.reciprocal(out=inv_std[:], in_=std_of_group[g][:])
+            nc.vector.bn_aggr(out=mean_var[:], in_=stats_of_group[g][:])
+            nc.scalar.activation(
+                out=inv_std[:], in_=mean_var[:, 1:2], func=ACT.Abs_reciprocal_sqrt, scale=PATCH / (PATCH - 1.0)
+            )
             inv_std_of_group[g] = inv_std
 
         def normalise(g):
@@ -192,8 +188,6 @@ def tile_norm_conv_s_kernel(tc, a, conv_kernel, out):
                 normalise(measured)
             if step < GROUPS:
                 spread(step)
-            if 0 <= step - 1 < GROUPS:
-                invert(step - 1)
             if 0 <= measured < GROUPS:
                 if measured % 2 == 1:
                     channels_onto_partitions(measured // 2)

@@ -23,6 +23,8 @@ ROUNDS = SIDE // ROUND_ROWS
 GROUPS = 2 * ROUNDS
 ROUND_PIXELS = ROUND_ROWS * SIDE
 PADDED = (SIDE + 1) * SIDE
+TOP_ROWS = ROUND_ROWS + 1
+TOP = TOP_ROWS * SIDE
 BANK = 512
 GROUP_WORDS = 2 * P
 PATCH_BANKS = 5
@@ -49,14 +51,18 @@ def tile_norm_conv_s_kernel(tc, a, conv_kernel, out):
         image = keep.tile([P, PADDED], BF16)
         shifted = keep.tile([P, PADDED], BF16)
         w_rows = keep.tile([P, TAPS, OUT_CH], BF16)
-        nc.sync.dma_start(out=image[:, SIDE:PADDED], in_=a_flat)
-        nc.sync.dma_start(out=shifted[:, SIDE + 1 : PADDED], in_=a_flat[:, 0 : PIXELS - 1])
+        nc.sync.dma_start(out=image[:, 0:SIDE], in_=a_flat[:, SIDE : 2 * SIDE])
+        nc.sync.dma_start(out=image[:, SIDE:TOP], in_=a_flat[:, 0 : TOP - SIDE])
+        nc.sync.dma_start(out=shifted[:, 0:SIDE], in_=a_flat[:, SIDE - 1 : 2 * SIDE - 1])
+        nc.sync.dma_start(out=shifted[:, SIDE + 1 : TOP], in_=a_flat[:, 0 : TOP - SIDE - 1])
+        nc.sync.dma_start(out=image[:, TOP:PADDED], in_=a_flat[:, TOP - SIDE : PIXELS])
+        nc.sync.dma_start(out=shifted[:, TOP:PADDED], in_=a_flat[:, TOP - SIDE - 1 : PIXELS - 1])
         nc.sync.dma_start(out=w_rows[:], in_=conv_kernel.rearrange("(c t) o -> c t o", t=TAPS))
 
         one = keep.tile([P, 1], F32)
         root_of_one = keep.tile([P, 1], F32)
         nc.vector.memset(one[:], 1.0)
-        nc.scalar.activation(out=root_of_one[:], in_=one[:], func=ACT.Abs_reciprocal_sqrt)
+        nc.scalar.activation(out=root_of_one[:], in_=one[:], func=ACT.Sqrt)
         minus_share = keep.tile([P, 1], BF16)
         nc.vector.memset(minus_share[:], -1.0 / PATCH)
 
@@ -65,9 +71,8 @@ def tile_norm_conv_s_kernel(tc, a, conv_kernel, out):
 
         image_rows = image[:].rearrange("c (r w) -> c r w", w=SIDE)
         shifted_rows = shifted[:].rearrange("c (r w) -> c r w", w=SIDE)
-        nc.vector.tensor_copy(out=image_rows[:, 0, :], in_=image_rows[:, 2, :])
-        nc.vector.tensor_copy(out=shifted_rows[:, 1:, 0:1], in_=image_rows[:, 1:, 1:2])
-        nc.vector.tensor_copy(out=shifted_rows[:, 0, :], in_=shifted_rows[:, 2, :])
+        for rows in (slice(0, TOP_ROWS), slice(TOP_ROWS, SIDE + 1)):
+            nc.gpsimd.tensor_copy(out=shifted_rows[:, rows, 0:1], in_=image_rows[:, rows, 1:2])
 
         w_grouped = keep.tile([P, OUT_CH, TAPS], BF16, align_bytes=64)
         w_codes = keep.tile([P, OUT_CH], U32, align_bytes=64)
@@ -84,6 +89,7 @@ def tile_norm_conv_s_kernel(tc, a, conv_kernel, out):
         source_of_parity = (shifted, image)
         patch_of_group = {}
         stats_of_group = {}
+        std_of_group = {}
         inv_std_of_group = {}
         normed_of_round = {}
         grouped_of_round = {}
@@ -117,11 +123,14 @@ def tile_norm_conv_s_kernel(tc, a, conv_kernel, out):
 
         def spread(g):
             mean_var = small.tile([P, 2], F32, name="mean_var")
-            inv_std = small.tile([P, 1], F32, name="inv_std")
+            std = small.tile([P, 1], F32, name="std")
             nc.vector.bn_aggr(out=mean_var[:], in_=stats_of_group[g][:])
-            nc.scalar.activation(
-                out=inv_std[:], in_=mean_var[:, 1:2], func=ACT.Abs_reciprocal_sqrt, scale=PATCH / (PATCH - 1.0)
-            )
+            nc.scalar.activation(out=std[:], in_=mean_var[:, 1:2], func=ACT.Sqrt, scale=PATCH / (PATCH - 1.0))
+            std_of_group[g] = std
+
+        def invert(g):
+            inv_std = small.tile([P, 1], F32, name="inv_std")
+            nc.vector.reciprocal(out=inv_std[:], in_=std_of_group[g][:])
             inv_std_of_group[g] = inv_std
 
         def normalise(g):
@@ -175,7 +184,10 @@ def tile_norm_conv_s_kernel(tc, a, conv_kernel, out):
             pixels = slice(ROUND_PIXELS * r, ROUND_PIXELS * (r + 1))
             for pair in range(2):
                 result = results.tile([P, 2, ROUND_PIXELS], F32, name="result")
-                nc.scalar.copy(out=result[:], in_=products_of_round[r, pair][:])
+                if r == ROUNDS - 1 and pair == 1:
+                    nc.vector.tensor_copy(out=result[:], in_=products_of_round[r, pair][:])
+                else:
+                    nc.scalar.copy(out=result[:], in_=products_of_round[r, pair][:])
                 nc.sync.dma_start(out=out_view[:, 2 * pair : 2 * pair + 2, pixels], in_=result[:])
 
         for g in range(PATCH_BANKS):
@@ -188,6 +200,8 @@ def tile_norm_conv_s_kernel(tc, a, conv_kernel, out):
                 normalise(measured)
             if step < GROUPS:
                 spread(step)
+            if 0 <= step - 1 < GROUPS:
+                invert(step - 1)
             if 0 <= measured < GROUPS:
                 if measured % 2 == 1:
                     channels_onto_partitions(measured // 2)

@@ -29,6 +29,7 @@ BANK = 512
 GROUP_WORDS = 2 * P
 PATCH_BANKS = 5
 LAG = 2
+WARM_UP = 3
 
 FLOPS = 2 * PIXELS * PATCH * OUT_CH
 
@@ -42,7 +43,7 @@ def tile_norm_conv_s_kernel(tc, a, conv_kernel, out):
         keep = ctx.enter_context(tc.tile_pool(name="keep", bufs=1))
         small = ctx.enter_context(tc.tile_pool(name="small", bufs=PATCH_BANKS))
         work = ctx.enter_context(tc.tile_pool(name="work", bufs=2))
-        results = ctx.enter_context(tc.tile_pool(name="results", bufs=4))
+        results = ctx.enter_context(tc.tile_pool(name="results", bufs=2 * ROUNDS))
         psum_patch = ctx.enter_context(tc.psum_pool(name="psum_patch", bufs=PATCH_BANKS))
         psum_back = ctx.enter_context(tc.psum_pool(name="psum_back", bufs=1))
         psum_out = ctx.enter_context(tc.psum_pool(name="psum_out", bufs=2))
@@ -62,12 +63,20 @@ def tile_norm_conv_s_kernel(tc, a, conv_kernel, out):
         one = keep.tile([P, 1], F32)
         root_of_one = keep.tile([P, 1], F32)
         nc.vector.memset(one[:], 1.0)
-        nc.scalar.activation(out=root_of_one[:], in_=one[:], func=ACT.Sqrt)
+        nc.scalar.activation(out=root_of_one[:], in_=one[:], func=ACT.Abs_reciprocal_sqrt)
         minus_share = keep.tile([P, 1], BF16)
         nc.vector.memset(minus_share[:], -1.0 / PATCH)
 
         identity = keep.tile([P, P], F32)
         make_identity(nc, identity[:])
+
+        zeros = keep.tile([P, BANK], BF16)
+        nc.vector.memset(zeros[:], 0.0)
+        warm = psum_out.tile([P, 2, ROUND_PIXELS], F32, name="acc")
+        for turn in range(WARM_UP):
+            nc.tensor.matmul(
+                out=warm[:].rearrange("p t x -> p (t x)"), lhsT=zeros[:, 0:P], rhs=zeros[:], start=True, stop=True
+            )
 
         image_rows = image[:].rearrange("c (r w) -> c r w", w=SIDE)
         shifted_rows = shifted[:].rearrange("c (r w) -> c r w", w=SIDE)
@@ -89,7 +98,7 @@ def tile_norm_conv_s_kernel(tc, a, conv_kernel, out):
         source_of_parity = (shifted, image)
         patch_of_group = {}
         stats_of_group = {}
-        std_of_group = {}
+        stats_of_round = {}
         inv_std_of_group = {}
         normed_of_round = {}
         grouped_of_round = {}
@@ -99,11 +108,16 @@ def tile_norm_conv_s_kernel(tc, a, conv_kernel, out):
             r, parity = g // 2, (g + 1) % 2
             source = source_of_parity[parity]
             words = source[:].bitcast(F32)
-            pairs = source[:].rearrange("c (x kw) -> c x kw", kw=2)
             patch = psum_patch.tile([P, BANK], F32, name="patch")
             for kh in range(2):
                 first = (ROUND_ROWS * r + kh) * ROW_WORDS
                 nc.tensor.transpose(patch[:, P * kh : P * (kh + 1)], words[:, first : first + P], identity[:])
+            patch_of_group[g] = patch
+
+        def sum_patches(g):
+            r, parity = g // 2, (g + 1) % 2
+            pairs = source_of_parity[parity][:].rearrange("c (x kw) -> c x kw", kw=2)
+            patch = patch_of_group[g]
             for tap in range(TAPS):
                 kh, kw = divmod(tap, 2)
                 first = (ROUND_ROWS * r + kh) * ROW_WORDS
@@ -114,23 +128,25 @@ def tile_norm_conv_s_kernel(tc, a, conv_kernel, out):
                     start=(tap == 0),
                     stop=(tap == TAPS - 1),
                 )
-            patch_of_group[g] = patch
 
         def measure(g):
-            stats = small.tile([P, 6], F32, name="stats")
-            nc.vector.bn_stats(out=stats[:], in_=patch_of_group[g][:].bitcast(BF16)[:, 0:PATCH])
-            stats_of_group[g] = stats
+            values = patch_of_group[g][:].bitcast(BF16)
+            if g % 2 == 0:
+                stats = small.tile([P, 12], F32, name="stats")
+                nc.vector.bn_stats(out=stats[:, 6:12], in_=values[:, 0:PATCH])
+                stats_of_group[g] = stats[:, 6:12]
+                stats_of_group[g + 1] = stats[:, 0:9]
+                stats_of_round[g // 2] = stats
+            else:
+                nc.vector.bn_stats(out=stats_of_round[g // 2][:, 0:6], in_=values[:, 0:PATCH:2])
 
         def spread(g):
             mean_var = small.tile([P, 2], F32, name="mean_var")
-            std = small.tile([P, 1], F32, name="std")
-            nc.vector.bn_aggr(out=mean_var[:], in_=stats_of_group[g][:])
-            nc.scalar.activation(out=std[:], in_=mean_var[:, 1:2], func=ACT.Sqrt, scale=PATCH / (PATCH - 1.0))
-            std_of_group[g] = std
-
-        def invert(g):
             inv_std = small.tile([P, 1], F32, name="inv_std")
-            nc.vector.reciprocal(out=inv_std[:], in_=std_of_group[g][:])
+            nc.vector.bn_aggr(out=mean_var[:], in_=stats_of_group[g])
+            nc.scalar.activation(
+                out=inv_std[:], in_=mean_var[:, 1:2], func=ACT.Abs_reciprocal_sqrt, scale=PATCH / (PATCH - 1.0)
+            )
             inv_std_of_group[g] = inv_std
 
         def normalise(g):
@@ -195,13 +211,12 @@ def tile_norm_conv_s_kernel(tc, a, conv_kernel, out):
         for step in range(GROUPS + 2 * LAG + 1):
             if step < GROUPS:
                 measure(step)
+                sum_patches(step)
             measured = step - LAG
             if 0 <= measured < GROUPS:
                 normalise(measured)
             if step < GROUPS:
                 spread(step)
-            if 0 <= step - 1 < GROUPS:
-                invert(step - 1)
             if 0 <= measured < GROUPS:
                 if measured % 2 == 1:
                     channels_onto_partitions(measured // 2)

@@ -25,11 +25,12 @@ ROUND_PIXELS = ROUND_ROWS * SIDE
 PADDED = (SIDE + 1) * SIDE
 TOP_ROWS = ROUND_ROWS + 1
 TOP = TOP_ROWS * SIDE
+W_HALVES = (slice(0, OUT_CH // 2), slice(OUT_CH // 2, OUT_CH))
 BANK = 512
 GROUP_WORDS = 2 * P
 PATCH_BANKS = 5
 LAG = 2
-WARM_UP = 3
+WARM_UP = 10
 
 FLOPS = 2 * PIXELS * PATCH * OUT_CH
 
@@ -41,7 +42,7 @@ def tile_norm_conv_s_kernel(tc, a, conv_kernel, out):
 
     with ExitStack() as ctx:
         keep = ctx.enter_context(tc.tile_pool(name="keep", bufs=1))
-        small = ctx.enter_context(tc.tile_pool(name="small", bufs=PATCH_BANKS))
+        small = ctx.enter_context(tc.tile_pool(name="small", bufs=GROUPS))
         work = ctx.enter_context(tc.tile_pool(name="work", bufs=2))
         results = ctx.enter_context(tc.tile_pool(name="results", bufs=2 * ROUNDS))
         psum_patch = ctx.enter_context(tc.psum_pool(name="psum_patch", bufs=PATCH_BANKS))
@@ -58,7 +59,9 @@ def tile_norm_conv_s_kernel(tc, a, conv_kernel, out):
         nc.sync.dma_start(out=shifted[:, SIDE + 1 : TOP], in_=a_flat[:, 0 : TOP - SIDE - 1])
         nc.sync.dma_start(out=image[:, TOP:PADDED], in_=a_flat[:, TOP - SIDE : PIXELS])
         nc.sync.dma_start(out=shifted[:, TOP:PADDED], in_=a_flat[:, TOP - SIDE - 1 : PIXELS - 1])
-        nc.sync.dma_start(out=w_rows[:], in_=conv_kernel.rearrange("(c t) o -> c t o", t=TAPS))
+        w_view = conv_kernel.rearrange("(c t) o -> c t o", t=TAPS)
+        for half in W_HALVES:
+            nc.sync.dma_start(out=w_rows[:, :, half], in_=w_view[:, :, half])
 
         one = keep.tile([P, 1], F32)
         root_of_one = keep.tile([P, 1], F32)
@@ -69,14 +72,11 @@ def tile_norm_conv_s_kernel(tc, a, conv_kernel, out):
 
         identity = keep.tile([P, P], F32)
         make_identity(nc, identity[:])
-
-        zeros = keep.tile([P, BANK], BF16)
+        zeros = keep.tile([P, P], BF16)
         nc.vector.memset(zeros[:], 0.0)
         warm = psum_out.tile([P, 2, ROUND_PIXELS], F32, name="acc")
         for turn in range(WARM_UP):
-            nc.tensor.matmul(
-                out=warm[:].rearrange("p t x -> p (t x)"), lhsT=zeros[:, 0:P], rhs=zeros[:], start=True, stop=True
-            )
+            nc.tensor.matmul(out=warm[:, 0, 0:P], lhsT=zeros[:], rhs=zeros[:], start=True, stop=True)
 
         image_rows = image[:].rearrange("c (r w) -> c r w", w=SIDE)
         shifted_rows = shifted[:].rearrange("c (r w) -> c r w", w=SIDE)
@@ -86,21 +86,25 @@ def tile_norm_conv_s_kernel(tc, a, conv_kernel, out):
         w_grouped = keep.tile([P, OUT_CH, TAPS], BF16, align_bytes=64)
         w_codes = keep.tile([P, OUT_CH], U32, align_bytes=64)
         w_scales = keep.tile([P, OUT_CH], U8, align_bytes=64)
-        nc.gpsimd.tensor_scalar(
-            out=w_grouped[:],
-            in0=w_rows[:].rearrange("c t o -> c o t"),
-            scalar1=1.0,
-            scalar2=0.0,
-            op0=ALU.mult,
-            op1=ALU.add,
-        )
+        for half in W_HALVES:
+            nc.gpsimd.tensor_scalar(
+                out=w_grouped[:, half, :],
+                in0=w_rows[:, :, half].rearrange("c t o -> c o t"),
+                scalar1=1.0,
+                scalar2=0.0,
+                op0=ALU.mult,
+                op1=ALU.add,
+            )
 
         source_of_parity = (shifted, image)
         patch_of_group = {}
         stats_of_group = {}
         stats_of_round = {}
+        mean_var_of_group = {}
         inv_std_of_group = {}
         normed_of_round = {}
+        back_of_round = {}
+        quantised_of_round = {}
         grouped_of_round = {}
         products_of_round = {}
 
@@ -142,8 +146,12 @@ def tile_norm_conv_s_kernel(tc, a, conv_kernel, out):
 
         def spread(g):
             mean_var = small.tile([P, 2], F32, name="mean_var")
-            inv_std = small.tile([P, 1], F32, name="inv_std")
             nc.vector.bn_aggr(out=mean_var[:], in_=stats_of_group[g])
+            mean_var_of_group[g] = mean_var
+
+        def root(g):
+            mean_var = mean_var_of_group[g]
+            inv_std = small.tile([P, 1], F32, name="inv_std")
             nc.scalar.activation(
                 out=inv_std[:], in_=mean_var[:, 1:2], func=ACT.Abs_reciprocal_sqrt, scale=PATCH / (PATCH - 1.0)
             )
@@ -170,6 +178,10 @@ def tile_norm_conv_s_kernel(tc, a, conv_kernel, out):
             for slot in range(4):
                 cols = slice(P * slot, P * (slot + 1))
                 nc.tensor.transpose(back[:, cols], normed_words[:, cols], identity[:])
+            back_of_round[r] = back
+
+        def regroup(r):
+            back = back_of_round[r]
             grouped = work.tile([P, ROUND_PIXELS * TAPS], BF16, name="grouped", align_bytes=64)
             nc.scalar.copy(
                 out=grouped[:].bitcast(F32).rearrange("c (q s k) -> c q s k", s=2, k=2),
@@ -177,59 +189,169 @@ def tile_norm_conv_s_kernel(tc, a, conv_kernel, out):
             )
             grouped_of_round[r] = grouped
 
-        def multiply(r):
+        def half_onto_partitions(r, slot):
+            normed_words = normed_of_round[r][:, PATCH * (1 - slot) : PATCH * (2 - slot)].bitcast(F32)
+            back = psum_patch.tile([P, BANK], F32, name="patch")
+            for kh in range(2):
+                cols = slice(P * kh, P * (kh + 1))
+                nc.tensor.transpose(back[:, cols], normed_words[:, cols], identity[:])
+            back_of_round[r, slot] = back
+
+        def regroup_half(r, slot, on_vector):
+            grouped = work.tile([P, PATCH], BF16, name="grouped_half", align_bytes=64)
+            ordered = grouped[:].bitcast(F32).rearrange("c (q k) -> c q k", k=2)
+            words = back_of_round[r, slot][:, 0:GROUP_WORDS].rearrange("c (k q) -> c q k", k=2)
+            if on_vector:
+                nc.vector.tensor_copy(out=ordered, in_=words)
+            else:
+                nc.scalar.copy(out=ordered, in_=words)
+            grouped_of_round[r, slot] = grouped
+
+        def quantise_half(r, slot):
+            x_codes = work.tile([P, P], U32, name="x_codes_half", align_bytes=64)
+            x_scales = work.tile([P, P], U8, name="x_scales_half", align_bytes=64)
+            nc.vector.quantize_mx(out=x_codes[:].bitcast(FP8X4), scales=x_scales[:], in_=grouped_of_round[r, slot][:])
+            quantised_of_round[r, slot] = x_codes, x_scales
+
+        def multiply_half(r, pair, slot):
+            if slot == 0:
+                products_of_round[r, pair] = psum_patch.tile([P, BANK], F32, name="patch")
+            acc = products_of_round[r, pair]
+            x_codes, x_scales = quantised_of_round[r, slot]
+            for half in range(2):
+                o_cols = slice(P * (2 * pair + half), P * (2 * pair + half + 1))
+                nc.tensor.matmul_mx(
+                    out=acc[:, ROUND_PIXELS * half + P * (1 - slot) : ROUND_PIXELS * half + P * (2 - slot)],
+                    lhsT=w_codes[:, o_cols].bitcast(FP8X4),
+                    lhsT_scale=w_scales[:, o_cols],
+                    rhs=x_codes[:].bitcast(FP8X4),
+                    rhs_scale=x_scales[:],
+                    start=True,
+                    stop=True,
+                )
+
+        def store_quarter(r, pair, half, on_vector):
+            pixels = slice(ROUND_PIXELS * r, ROUND_PIXELS * (r + 1))
+            result = results.tile([P, ROUND_PIXELS], F32, name="result_quarter")
+            products = products_of_round[r, pair][:, ROUND_PIXELS * half : ROUND_PIXELS * (half + 1)]
+            in_order = products.rearrange("p (s q) -> p q s", s=2)
+            ordered = result[:].rearrange("p (q s) -> p q s", s=2)
+            if on_vector:
+                nc.vector.tensor_copy(out=ordered, in_=in_order)
+            else:
+                nc.scalar.copy(out=ordered, in_=in_order)
+            nc.sync.dma_start(out=out_view[:, 2 * pair + half, pixels], in_=result[:])
+
+        def quantise(r):
             x_codes = work.tile([P, ROUND_PIXELS], U32, name="x_codes", align_bytes=64)
             x_scales = work.tile([P, ROUND_PIXELS], U8, name="x_scales", align_bytes=64)
             nc.vector.quantize_mx(out=x_codes[:].bitcast(FP8X4), scales=x_scales[:], in_=grouped_of_round[r][:])
-            for pair in range(2):
-                acc = psum_out.tile([P, 2, ROUND_PIXELS], F32, name="acc")
-                for half in range(2):
-                    o_cols = slice(P * (2 * pair + half), P * (2 * pair + half + 1))
-                    nc.tensor.matmul_mx(
-                        out=acc[:, half, :],
-                        lhsT=w_codes[:, o_cols].bitcast(FP8X4),
-                        lhsT_scale=w_scales[:, o_cols],
-                        rhs=x_codes[:].bitcast(FP8X4),
-                        rhs_scale=x_scales[:],
-                        start=True,
-                        stop=True,
-                    )
-                products_of_round[r, pair] = acc
+            quantised_of_round[r] = x_codes, x_scales
 
-        def store(r):
-            pixels = slice(ROUND_PIXELS * r, ROUND_PIXELS * (r + 1))
-            for pair in range(2):
-                result = results.tile([P, 2, ROUND_PIXELS], F32, name="result")
-                if r == ROUNDS - 1 and pair == 1:
-                    nc.vector.tensor_copy(out=result[:], in_=products_of_round[r, pair][:])
-                else:
-                    nc.scalar.copy(out=result[:], in_=products_of_round[r, pair][:])
-                nc.sync.dma_start(out=out_view[:, 2 * pair : 2 * pair + 2, pixels], in_=result[:])
-
-        for g in range(PATCH_BANKS):
-            pixels_onto_partitions(g)
-        for step in range(GROUPS + 2 * LAG + 1):
-            if step < GROUPS:
-                measure(step)
-                sum_patches(step)
-            measured = step - LAG
-            if 0 <= measured < GROUPS:
-                normalise(measured)
-            if step < GROUPS:
-                spread(step)
-            if 0 <= measured < GROUPS:
-                if measured % 2 == 1:
-                    channels_onto_partitions(measured // 2)
-                if measured + PATCH_BANKS < GROUPS:
-                    pixels_onto_partitions(measured + PATCH_BANKS)
-            if step == 2 * LAG:
-                nc.vector.quantize_mx(
-                    out=w_codes[:].bitcast(FP8X4),
-                    scales=w_scales[:],
-                    in_=w_grouped[:].rearrange("c o t -> c (o t)"),
+        def multiply(r, pair):
+            x_codes, x_scales = quantised_of_round[r]
+            acc = psum_out.tile([P, 2, ROUND_PIXELS], F32, name="acc")
+            for half in range(2):
+                o_cols = slice(P * (2 * pair + half), P * (2 * pair + half + 1))
+                nc.tensor.matmul_mx(
+                    out=acc[:, half, :],
+                    lhsT=w_codes[:, o_cols].bitcast(FP8X4),
+                    lhsT_scale=w_scales[:, o_cols],
+                    rhs=x_codes[:].bitcast(FP8X4),
+                    rhs_scale=x_scales[:],
+                    start=True,
+                    stop=True,
                 )
-            turned = step - 2 * LAG
-            if 0 <= turned < GROUPS and turned % 2 == 1:
-                multiply(turned // 2)
-            if 0 <= turned - 1 < GROUPS and (turned - 1) % 2 == 1:
-                store((turned - 1) // 2)
+            products_of_round[r, pair] = acc
+
+        def store(r, pair, on_vector=False):
+            pixels = slice(ROUND_PIXELS * r, ROUND_PIXELS * (r + 1))
+            result = results.tile([P, 2, ROUND_PIXELS], F32, name="result")
+            if on_vector:
+                nc.vector.tensor_copy(out=result[:], in_=products_of_round[r, pair][:])
+            else:
+                nc.scalar.copy(out=result[:], in_=products_of_round[r, pair][:])
+            nc.sync.dma_start(out=out_view[:, 2 * pair : 2 * pair + 2, pixels], in_=result[:])
+
+        def quantise_weights(half):
+            nc.vector.quantize_mx(
+                out=w_codes[:, half].bitcast(FP8X4),
+                scales=w_scales[:, half],
+                in_=w_grouped[:, half, :].rearrange("c o t -> c (o t)"),
+            )
+
+        def begin(g):
+            measure(g)
+            sum_patches(g)
+
+        def finish_stats(g):
+            spread(g)
+            root(g)
+
+        pixels_onto_partitions(0)
+        pixels_onto_partitions(1)
+        pixels_onto_partitions(2)
+        begin(0)
+        finish_stats(0)
+        begin(1)
+        pixels_onto_partitions(3)
+        begin(2)
+        finish_stats(1)
+        finish_stats(2)
+        pixels_onto_partitions(4)
+        normalise(0)
+        begin(3)
+        normalise(1)
+        channels_onto_partitions(0)
+        pixels_onto_partitions(5)
+        begin(4)
+        finish_stats(3)
+        finish_stats(4)
+        pixels_onto_partitions(6)
+        normalise(2)
+        regroup(0)
+        begin(5)
+        normalise(3)
+        finish_stats(5)
+        channels_onto_partitions(1)
+        pixels_onto_partitions(7)
+        quantise_weights(W_HALVES[0])
+        quantise(0)
+        multiply(0, 0)
+        quantise_weights(W_HALVES[1])
+        multiply(0, 1)
+        regroup(1)
+        store(0, 0)
+        store(0, 1)
+        normalise(4)
+        normalise(5)
+        channels_onto_partitions(2)
+        begin(6)
+        begin(7)
+        finish_stats(6)
+        finish_stats(7)
+        regroup(2)
+        quantise(1)
+        multiply(1, 0)
+        multiply(1, 1)
+        normalise(6)
+        half_onto_partitions(3, 0)
+        normalise(7)
+        half_onto_partitions(3, 1)
+        store(1, 0)
+        quantise(2)
+        multiply(2, 0)
+        store(1, 1, True)
+        multiply(2, 1)
+        regroup_half(3, 0, False)
+        regroup_half(3, 1, False)
+        quantise_half(3, 0)
+        quantise_half(3, 1)
+        store(2, 1, True)
+        store(2, 0)
+        for slot in range(2):
+            for pair in range(2):
+                multiply_half(3, pair, slot)
+        for half in range(2):
+            store_quarter(3, 0, half, False)
+            store_quarter(3, 1, half, True)

@@ -326,29 +326,29 @@ def tile_norm_conv_s_kernel(tc, a, conv_kernel, out):
         normalise(4)
         normalise(5)
         channels_onto_partitions(2)
-        begin(6)
-        begin(7)
-        finish_stats(6)
-        finish_stats(7)
         regroup(2)
         quantise(1)
         multiply(1, 0)
         multiply(1, 1)
+        begin(6)
+        begin(7)
+        finish_stats(6)
+        finish_stats(7)
+        store(1, 0)
+        store(1, 1)
+        quantise(2)
+        multiply(2, 0)
         normalise(6)
         half_onto_partitions(3, 0)
         normalise(7)
         half_onto_partitions(3, 1)
-        store(1, 0)
-        quantise(2)
-        multiply(2, 0)
-        store(1, 1, True)
         multiply(2, 1)
         regroup_half(3, 0, False)
         regroup_half(3, 1, False)
+        store(2, 0, True)
         quantise_half(3, 0)
         quantise_half(3, 1)
-        store(2, 1, True)
-        store(2, 0)
+        store(2, 1)
         for slot in range(2):
             for pair in range(2):
                 multiply_half(3, pair, slot)

@@ -74,9 +74,15 @@ def tile_norm_conv_s_kernel(tc, a, conv_kernel, out):
         make_identity(nc, identity[:])
         zeros = keep.tile([P, P], BF16)
         nc.vector.memset(zeros[:], 0.0)
-        warm = psum_out.tile([P, 2, ROUND_PIXELS], F32, name="acc")
+        warm = psum_out.tile([P, BANK], F32, name="acc")
         for turn in range(WARM_UP):
-            nc.tensor.matmul(out=warm[:, 0, 0:P], lhsT=zeros[:], rhs=zeros[:], start=True, stop=True)
+            nc.tensor.matmul(out=warm[:, 0:P], lhsT=zeros[:], rhs=zeros[:], start=True, stop=True)
+
+        neighbour = keep.tile([P, P], F32)
+        from_rows = identity[:].rearrange("k (i m) -> k i m", m=ROW_WORDS)
+        to_rows = neighbour[:].rearrange("k (i m) -> k i m", m=ROW_WORDS)
+        nc.gpsimd.tensor_copy(out=to_rows[:, :, 1:ROW_WORDS], in_=from_rows[:, :, 0 : ROW_WORDS - 1])
+        nc.gpsimd.tensor_copy(out=to_rows[:, :, 0:1], in_=from_rows[:, :, 0:1])
 
         image_rows = image[:].rearrange("c (r w) -> c r w", w=SIDE)
         shifted_rows = shifted[:].rearrange("c (r w) -> c r w", w=SIDE)
@@ -100,6 +106,9 @@ def tile_norm_conv_s_kernel(tc, a, conv_kernel, out):
         patch_of_group = {}
         stats_of_group = {}
         stats_of_round = {}
+        moved_of_round = {}
+        minus_mean_of_group = {}
+        deviation_of_group = {}
         mean_var_of_group = {}
         inv_std_of_group = {}
         normed_of_round = {}
@@ -132,6 +141,41 @@ def tile_norm_conv_s_kernel(tc, a, conv_kernel, out):
                     start=(tap == 0),
                     stop=(tap == TAPS - 1),
                 )
+
+        def fetch_mean(g):
+            minus_mean = small.tile([P, 1], F32, name="minus_mean")
+            nc.scalar.copy(out=minus_mean[:], in_=patch_of_group[g][:, GROUP_WORDS : GROUP_WORDS + 1])
+            minus_mean_of_group[g] = minus_mean
+
+        def square(g):
+            squares = work.tile([P, PATCH], BF16, name="squares")
+            deviation = small.tile([P, 1], F32, name="deviation")
+            nc.scalar.activation(
+                out=squares[:],
+                in_=patch_of_group[g][:].bitcast(BF16)[:, 0:PATCH],
+                func=ACT.Square,
+                bias=minus_mean_of_group[g][:],
+                accum_out=deviation[:],
+            )
+            deviation_of_group[g] = deviation
+
+        def root_of_square(g):
+            inv_std = small.tile([P, 1], F32, name="inv_std")
+            nc.scalar.activation(
+                out=inv_std[:], in_=deviation_of_group[g][:], func=ACT.Abs_reciprocal_sqrt, scale=1.0 / (PATCH - 1.0)
+            )
+            inv_std_of_group[g] = inv_std
+
+        def move_left_column(r):
+            stats = stats_of_round[r]
+            moved = patch_of_group[2 * r + 1][:, GROUP_WORDS + 1 : GROUP_WORDS + 4]
+            nc.tensor.matmul(out=moved, lhsT=neighbour[:], rhs=stats[:, 9:12], start=True, stop=True)
+            moved_of_round[r] = moved
+
+        def fetch_left_column(r):
+            stats = stats_of_round[r]
+            nc.scalar.copy(out=stats[:, 3:6], in_=moved_of_round[r])
+            stats_of_group[2 * r + 1] = stats[:, 3:9]
 
         def measure(g):
             values = patch_of_group[g][:].bitcast(BF16)
@@ -191,7 +235,12 @@ def tile_norm_conv_s_kernel(tc, a, conv_kernel, out):
 
         def half_onto_partitions(r, slot):
             normed_words = normed_of_round[r][:, PATCH * (1 - slot) : PATCH * (2 - slot)].bitcast(F32)
-            back = psum_patch.tile([P, BANK], F32, name="patch")
+            if r == 0 and slot == 0:
+                back = psum_back.tile([P, BANK], F32, name="back")
+            elif r == 0:
+                back = psum_out.tile([P, BANK], F32, name="acc")
+            else:
+                back = psum_patch.tile([P, BANK], F32, name="patch")
             for kh in range(2):
                 cols = slice(P * kh, P * (kh + 1))
                 nc.tensor.transpose(back[:, cols], normed_words[:, cols], identity[:])
@@ -213,9 +262,16 @@ def tile_norm_conv_s_kernel(tc, a, conv_kernel, out):
             nc.vector.quantize_mx(out=x_codes[:].bitcast(FP8X4), scales=x_scales[:], in_=grouped_of_round[r, slot][:])
             quantised_of_round[r, slot] = x_codes, x_scales
 
+        def half_bank(r):
+            if r == 0:
+                bank = psum_out.tile([P, BANK], F32, name="acc")
+            else:
+                bank = psum_patch.tile([P, BANK], F32, name="patch")
+            return bank
+
         def multiply_half(r, pair, slot):
             if slot == 0:
-                products_of_round[r, pair] = psum_patch.tile([P, BANK], F32, name="patch")
+                products_of_round[r, pair] = half_bank(r)
             acc = products_of_round[r, pair]
             x_codes, x_scales = quantised_of_round[r, slot]
             for half in range(2):
@@ -250,11 +306,11 @@ def tile_norm_conv_s_kernel(tc, a, conv_kernel, out):
 
         def multiply(r, pair):
             x_codes, x_scales = quantised_of_round[r]
-            acc = psum_out.tile([P, 2, ROUND_PIXELS], F32, name="acc")
+            acc = psum_out.tile([P, BANK], F32, name="acc")
             for half in range(2):
                 o_cols = slice(P * (2 * pair + half), P * (2 * pair + half + 1))
                 nc.tensor.matmul_mx(
-                    out=acc[:, half, :],
+                    out=acc[:, ROUND_PIXELS * half : ROUND_PIXELS * (half + 1)],
                     lhsT=w_codes[:, o_cols].bitcast(FP8X4),
                     lhsT_scale=w_scales[:, o_cols],
                     rhs=x_codes[:].bitcast(FP8X4),
@@ -266,12 +322,12 @@ def tile_norm_conv_s_kernel(tc, a, conv_kernel, out):
 
         def store(r, pair, on_vector=False):
             pixels = slice(ROUND_PIXELS * r, ROUND_PIXELS * (r + 1))
-            result = results.tile([P, 2, ROUND_PIXELS], F32, name="result")
+            result = results.tile([P, BANK], F32, name="result")
             if on_vector:
                 nc.vector.tensor_copy(out=result[:], in_=products_of_round[r, pair][:])
             else:
                 nc.scalar.copy(out=result[:], in_=products_of_round[r, pair][:])
-            nc.sync.dma_start(out=out_view[:, 2 * pair : 2 * pair + 2, pixels], in_=result[:])
+            nc.sync.dma_start(out=out_view[:, 2 * pair : 2 * pair + 2, pixels], in_=result[:].rearrange("p (t x) -> p t x", t=2))
 
         def quantise_weights(half):
             nc.vector.quantize_mx(
@@ -280,60 +336,75 @@ def tile_norm_conv_s_kernel(tc, a, conv_kernel, out):
                 in_=w_grouped[:, half, :].rearrange("c o t -> c (o t)"),
             )
 
-        def begin(g):
-            measure(g)
-            sum_patches(g)
-
-        def finish_stats(g):
-            spread(g)
-            root(g)
-
         pixels_onto_partitions(0)
+        measure(0)
         pixels_onto_partitions(1)
         pixels_onto_partitions(2)
-        begin(0)
-        finish_stats(0)
-        begin(1)
+        sum_patches(1)
+        sum_patches(0)
+        spread(0)
+        root(0)
+        fetch_mean(1)
+        square(1)
+        measure(2)
         pixels_onto_partitions(3)
-        begin(2)
-        finish_stats(1)
-        finish_stats(2)
         pixels_onto_partitions(4)
+        sum_patches(3)
         normalise(0)
-        begin(3)
-        normalise(1)
-        channels_onto_partitions(0)
+        half_onto_partitions(0, 0)
+        spread(2)
+        root(2)
+        root_of_square(1)
+        measure(4)
+        fetch_mean(3)
+        square(3)
+        sum_patches(2)
         pixels_onto_partitions(5)
-        begin(4)
-        finish_stats(3)
-        finish_stats(4)
-        pixels_onto_partitions(6)
+        normalise(1)
+        half_onto_partitions(0, 1)
+        spread(4)
+        root_of_square(3)
+        regroup_half(0, 0, False)
+        root(4)
+        sum_patches(4)
         normalise(2)
-        regroup(0)
-        begin(5)
+        measure(5)
+        pixels_onto_partitions(6)
         normalise(3)
-        finish_stats(5)
+        regroup_half(0, 1, False)
         channels_onto_partitions(1)
-        pixels_onto_partitions(7)
+        sum_patches(5)
+        quantise_half(0, 0)
+        spread(5)
+        root(5)
         quantise_weights(W_HALVES[0])
-        quantise(0)
-        multiply(0, 0)
+        quantise_half(0, 1)
+        multiply_half(0, 0, 0)
+        multiply_half(0, 0, 1)
         quantise_weights(W_HALVES[1])
-        multiply(0, 1)
+        multiply_half(0, 1, 0)
+        multiply_half(0, 1, 1)
+        pixels_onto_partitions(7)
         regroup(1)
-        store(0, 0)
-        store(0, 1)
+        store_quarter(0, 0, 0, False)
+        store_quarter(0, 0, 1, False)
+        store_quarter(0, 1, 0, False)
+        store_quarter(0, 1, 1, False)
         normalise(4)
         normalise(5)
         channels_onto_partitions(2)
-        regroup(2)
+        measure(6)
         quantise(1)
         multiply(1, 0)
         multiply(1, 1)
-        begin(6)
-        begin(7)
-        finish_stats(6)
-        finish_stats(7)
+        sum_patches(6)
+        regroup(2)
+        measure(7)
+        sum_patches(7)
+        spread(6)
+        root(6)
+        spread(7)
+        root(7)
         store(1, 0)
         store(1, 1)
         quantise(2)

@@ -55,10 +55,7 @@ def tile_norm_conv_s_kernel(tc, a, conv_kernel, out):
         w_rows = keep.tile([P, TAPS, OUT_CH], BF16)
         nc.sync.dma_start(out=image[:, 0:SIDE], in_=a_flat[:, SIDE : 2 * SIDE])
         nc.sync.dma_start(out=image[:, SIDE:TOP], in_=a_flat[:, 0 : TOP - SIDE])
-        nc.sync.dma_start(out=shifted[:, 0:SIDE], in_=a_flat[:, SIDE - 1 : 2 * SIDE - 1])
-        nc.sync.dma_start(out=shifted[:, SIDE + 1 : TOP], in_=a_flat[:, 0 : TOP - SIDE - 1])
         nc.sync.dma_start(out=image[:, TOP:PADDED], in_=a_flat[:, TOP - SIDE : PIXELS])
-        nc.sync.dma_start(out=shifted[:, TOP:PADDED], in_=a_flat[:, TOP - SIDE - 1 : PIXELS - 1])
         w_view = conv_kernel.rearrange("(c t) o -> c t o", t=TAPS)
         for half in W_HALVES:
             nc.sync.dma_start(out=w_rows[:, :, half], in_=w_view[:, :, half])
@@ -78,16 +75,12 @@ def tile_norm_conv_s_kernel(tc, a, conv_kernel, out):
         for turn in range(WARM_UP):
             nc.tensor.matmul(out=warm[:, 0:P], lhsT=zeros[:], rhs=zeros[:], start=True, stop=True)
 
-        neighbour = keep.tile([P, P], F32)
-        from_rows = identity[:].rearrange("k (i m) -> k i m", m=ROW_WORDS)
-        to_rows = neighbour[:].rearrange("k (i m) -> k i m", m=ROW_WORDS)
-        nc.gpsimd.tensor_copy(out=to_rows[:, :, 1:ROW_WORDS], in_=from_rows[:, :, 0 : ROW_WORDS - 1])
-        nc.gpsimd.tensor_copy(out=to_rows[:, :, 0:1], in_=from_rows[:, :, 0:1])
-
         image_rows = image[:].rearrange("c (r w) -> c r w", w=SIDE)
         shifted_rows = shifted[:].rearrange("c (r w) -> c r w", w=SIDE)
-        for rows in (slice(0, TOP_ROWS), slice(TOP_ROWS, SIDE + 1)):
-            nc.gpsimd.tensor_copy(out=shifted_rows[:, rows, 0:1], in_=image_rows[:, rows, 1:2])
+
+        def shift(copy, first, last):
+            copy(out=shifted_rows[:, first:last, 1:SIDE], in_=image_rows[:, first:last, 0 : SIDE - 1])
+            copy(out=shifted_rows[:, first:last, 0:1], in_=image_rows[:, first:last, 1:2])
 
         w_grouped = keep.tile([P, OUT_CH, TAPS], BF16, align_bytes=64)
         w_codes = keep.tile([P, OUT_CH], U32, align_bytes=64)
@@ -106,7 +99,6 @@ def tile_norm_conv_s_kernel(tc, a, conv_kernel, out):
         patch_of_group = {}
         stats_of_group = {}
         stats_of_round = {}
-        moved_of_round = {}
         minus_mean_of_group = {}
         deviation_of_group = {}
         mean_var_of_group = {}
@@ -165,17 +157,6 @@ def tile_norm_conv_s_kernel(tc, a, conv_kernel, out):
                 out=inv_std[:], in_=deviation_of_group[g][:], func=ACT.Abs_reciprocal_sqrt, scale=1.0 / (PATCH - 1.0)
             )
             inv_std_of_group[g] = inv_std
-
-        def move_left_column(r):
-            stats = stats_of_round[r]
-            moved = patch_of_group[2 * r + 1][:, GROUP_WORDS + 1 : GROUP_WORDS + 4]
-            nc.tensor.matmul(out=moved, lhsT=neighbour[:], rhs=stats[:, 9:12], start=True, stop=True)
-            moved_of_round[r] = moved
-
-        def fetch_left_column(r):
-            stats = stats_of_round[r]
-            nc.scalar.copy(out=stats[:, 3:6], in_=moved_of_round[r])
-            stats_of_group[2 * r + 1] = stats[:, 3:9]
 
         def measure(g):
             values = patch_of_group[g][:].bitcast(BF16)
@@ -337,7 +318,9 @@ def tile_norm_conv_s_kernel(tc, a, conv_kernel, out):
             )
 
         pixels_onto_partitions(0)
+        shift(nc.vector.tensor_copy, 0, TOP_ROWS)
         measure(0)
+        shift(nc.scalar.copy, TOP_ROWS, SIDE + 1)
         pixels_onto_partitions(1)
         pixels_onto_partitions(2)
         sum_patches(1)

@@ -30,7 +30,7 @@ BANK = 512
 GROUP_WORDS = 2 * P
 PATCH_BANKS = 5
 LAG = 2
-WARM_UP = 10
+WARM_UP = 3
 
 FLOPS = 2 * PIXELS * PATCH * OUT_CH
 
@@ -69,11 +69,15 @@ def tile_norm_conv_s_kernel(tc, a, conv_kernel, out):
 
         identity = keep.tile([P, P], F32)
         make_identity(nc, identity[:])
-        zeros = keep.tile([P, P], BF16)
+        zeros = keep.tile([P, P], F32)
         nc.vector.memset(zeros[:], 0.0)
         warm = psum_out.tile([P, BANK], F32, name="acc")
-        for turn in range(WARM_UP):
-            nc.tensor.matmul(out=warm[:, 0:P], lhsT=zeros[:], rhs=zeros[:], start=True, stop=True)
+
+        def keep_warm(turns):
+            for turn in range(turns):
+                nc.tensor.matmul(out=warm[:, 0:P], lhsT=zeros[:], rhs=zeros[:], start=True, stop=True)
+
+        keep_warm(WARM_UP)
 
         image_rows = image[:].rearrange("c (r w) -> c r w", w=SIDE)
         shifted_rows = shifted[:].rearrange("c (r w) -> c r w", w=SIDE)
@@ -318,11 +322,13 @@ def tile_norm_conv_s_kernel(tc, a, conv_kernel, out):
             )
 
         pixels_onto_partitions(0)
+        keep_warm(1)
         shift(nc.vector.tensor_copy, 0, TOP_ROWS)
         measure(0)
         shift(nc.scalar.copy, TOP_ROWS, SIDE + 1)
         pixels_onto_partitions(1)
         pixels_onto_partitions(2)
+        keep_warm(1)
         sum_patches(1)
         sum_patches(0)
         spread(0)
@@ -332,9 +338,11 @@ def tile_norm_conv_s_kernel(tc, a, conv_kernel, out):
         measure(2)
         pixels_onto_partitions(3)
         pixels_onto_partitions(4)
+        keep_warm(1)
         sum_patches(3)
         normalise(0)
         half_onto_partitions(0, 0)
+        keep_warm(1)
         spread(2)
         root(2)
         root_of_square(1)
@@ -345,6 +353,7 @@ def tile_norm_conv_s_kernel(tc, a, conv_kernel, out):
         pixels_onto_partitions(5)
         normalise(1)
         half_onto_partitions(0, 1)
+        keep_warm(1)
         spread(4)
         root_of_square(3)
         regroup_half(0, 0, False)

from contextlib import ExitStack

import concourse.mybir as mybir
from concourse.masks import make_identity

F32 = mybir.dt.float32
BF16 = mybir.dt.bfloat16
U32 = mybir.dt.uint32
U8 = mybir.dt.uint8
FP8X4 = mybir.dt.float8_e4m3fn_x4
ACT = mybir.ActivationFunctionType
ALU = mybir.AluOpType

P = 128
SIDE = 32
TAPS = 4
PATCH = P * TAPS
OUT_CH = 512
PIXELS = SIDE * SIDE
ROW_WORDS = SIDE // 2
ROUND_ROWS = P // ROW_WORDS
ROUNDS = SIDE // ROUND_ROWS
GROUPS = 2 * ROUNDS
ROUND_PIXELS = ROUND_ROWS * SIDE
PADDED = (SIDE + 1) * SIDE
TOP_ROWS = ROUND_ROWS + 1
TOP = TOP_ROWS * SIDE
W_HALVES = (slice(0, OUT_CH // 2), slice(OUT_CH // 2, OUT_CH))
BANK = 512
GROUP_WORDS = 2 * P
PATCH_BANKS = 5
LAG = 2
WARM_UP = 3

FLOPS = 2 * PIXELS * PATCH * OUT_CH


def tile_norm_conv_s_kernel(tc, a, conv_kernel, out):
    nc = tc.nc
    a_flat = a.rearrange("b c h w -> (b c) (h w)")
    out_view = out.rearrange("b (t p) h w -> p (b t) (h w)", p=P)

    with ExitStack() as ctx:
        keep = ctx.enter_context(tc.tile_pool(name="keep", bufs=1))
        small = ctx.enter_context(tc.tile_pool(name="small", bufs=GROUPS))
        work = ctx.enter_context(tc.tile_pool(name="work", bufs=2))
        results = ctx.enter_context(tc.tile_pool(name="results", bufs=2 * ROUNDS))
        psum_patch = ctx.enter_context(tc.psum_pool(name="psum_patch", bufs=PATCH_BANKS))
        psum_back = ctx.enter_context(tc.psum_pool(name="psum_back", bufs=1))
        psum_out = ctx.enter_context(tc.psum_pool(name="psum_out", bufs=2))
        ctx.enter_context(tc.manual_schedule())

        image = keep.tile([P, PADDED], BF16)
        shifted = keep.tile([P, PADDED], BF16)
        w_rows = keep.tile([P, TAPS, OUT_CH], BF16)
        nc.sync.dma_start(out=image[:, 0:SIDE], in_=a_flat[:, SIDE : 2 * SIDE])
        nc.sync.dma_start(out=image[:, SIDE:TOP], in_=a_flat[:, 0 : TOP - SIDE])
        nc.sync.dma_start(out=image[:, TOP:PADDED], in_=a_flat[:, TOP - SIDE : PIXELS])
        w_view = conv_kernel.rearrange("(c t) o -> c t o", t=TAPS)
        for half in W_HALVES:
            nc.sync.dma_start(out=w_rows[:, :, half], in_=w_view[:, :, half])

        one = keep.tile([P, 1], F32)
        root_of_one = keep.tile([P, 1], F32)
        nc.vector.memset(one[:], 1.0)
        nc.scalar.activation(out=root_of_one[:], in_=one[:], func=ACT.Abs_reciprocal_sqrt)
        minus_share = keep.tile([P, 1], BF16)
        nc.vector.memset(minus_share[:], -1.0 / PATCH)

        identity = keep.tile([P, P], F32)
        make_identity(nc, identity[:])
        zeros = keep.tile([P, P], F32)
        nc.vector.memset(zeros[:], 0.0)
        warm = psum_out.tile([P, BANK], F32, name="acc")

        def keep_warm(turns):
            for turn in range(turns):
                nc.tensor.matmul(out=warm[:, 0:P], lhsT=zeros[:], rhs=zeros[:], start=True, stop=True)

        keep_warm(WARM_UP)

        image_rows = image[:].rearrange("c (r w) -> c r w", w=SIDE)
        shifted_rows = shifted[:].rearrange("c (r w) -> c r w", w=SIDE)

        def shift(copy, first, last):
            copy(out=shifted_rows[:, first:last, 1:SIDE], in_=image_rows[:, first:last, 0 : SIDE - 1])
            copy(out=shifted_rows[:, first:last, 0:1], in_=image_rows[:, first:last, 1:2])

        w_grouped = keep.tile([P, OUT_CH, TAPS], BF16, align_bytes=64)
        w_codes = keep.tile([P, OUT_CH], U32, align_bytes=64)
        w_scales = keep.tile([P, OUT_CH], U8, align_bytes=64)
        for half in W_HALVES:
            nc.gpsimd.tensor_scalar(
                out=w_grouped[:, half, :],
                in0=w_rows[:, :, half].rearrange("c t o -> c o t"),
                scalar1=1.0,
                scalar2=0.0,
                op0=ALU.mult,
                op1=ALU.add,
            )

        source_of_parity = (shifted, image)
        patch_of_group = {}
        stats_of_group = {}
        stats_of_round = {}
        minus_mean_of_group = {}
        deviation_of_group = {}
        mean_var_of_group = {}
        inv_std_of_group = {}
        normed_of_round = {}
        back_of_round = {}
        quantised_of_round = {}
        grouped_of_round = {}
        products_of_round = {}

        def pixels_onto_partitions(g):
            r, parity = g // 2, (g + 1) % 2
            source = source_of_parity[parity]
            words = source[:].bitcast(F32)
            patch = psum_patch.tile([P, BANK], F32, name="patch")
            for kh in range(2):
                first = (ROUND_ROWS * r + kh) * ROW_WORDS
                nc.tensor.transpose(patch[:, P * kh : P * (kh + 1)], words[:, first : first + P], identity[:])
            patch_of_group[g] = patch

        def sum_patches(g):
            r, parity = g // 2, (g + 1) % 2
            pairs = source_of_parity[parity][:].rearrange("c (x kw) -> c x kw", kw=2)
            patch = patch_of_group[g]
            for tap in range(TAPS):
                kh, kw = divmod(tap, 2)
                first = (ROUND_ROWS * r + kh) * ROW_WORDS
                nc.tensor.matmul(
                    out=patch[:, GROUP_WORDS : GROUP_WORDS + 1],
                    lhsT=pairs[:, first : first + P, kw],
                    rhs=minus_share[:],
                    start=(tap == 0),
                    stop=(tap == TAPS - 1),
                )

        def fetch_mean(g):
            minus_mean = small.tile([P, 1], F32, name="minus_mean")
            nc.scalar.copy(out=minus_mean[:], in_=patch_of_group[g][:, GROUP_WORDS : GROUP_WORDS + 1])
            minus_mean_of_group[g] = minus_mean

        def square(g):
            squares = work.tile([P, PATCH], BF16, name="squares")
            deviation = small.tile([P, 1], F32, name="deviation")
            nc.scalar.activation(
                out=squares[:],
                in_=patch_of_group[g][:].bitcast(BF16)[:, 0:PATCH],
                func=ACT.Square,
                bias=minus_mean_of_group[g][:],
                accum_out=deviation[:],
            )
            deviation_of_group[g] = deviation

        def root_of_square(g):
            inv_std = small.tile([P, 1], F32, name="inv_std")
            nc.scalar.activation(
                out=inv_std[:], in_=deviation_of_group[g][:], func=ACT.Abs_reciprocal_sqrt, scale=1.0 / (PATCH - 1.0)
            )
            inv_std_of_group[g] = inv_std

        def measure(g):
            values = patch_of_group[g][:].bitcast(BF16)
            if g % 2 == 0:
                stats = small.tile([P, 12], F32, name="stats")
                nc.vector.bn_stats(out=stats[:, 6:12], in_=values[:, 0:PATCH])
                stats_of_group[g] = stats[:, 6:12]
                stats_of_group[g + 1] = stats[:, 0:9]
                stats_of_round[g // 2] = stats
            else:
                nc.vector.bn_stats(out=stats_of_round[g // 2][:, 0:6], in_=values[:, 0:PATCH:2])

        def spread(g):
            mean_var = small.tile([P, 2], F32, name="mean_var")
            nc.vector.bn_aggr(out=mean_var[:], in_=stats_of_group[g])
            mean_var_of_group[g] = mean_var

        def root(g):
            mean_var = mean_var_of_group[g]
            inv_std = small.tile([P, 1], F32, name="inv_std")
            nc.scalar.activation(
                out=inv_std[:], in_=mean_var[:, 1:2], func=ACT.Abs_reciprocal_sqrt, scale=PATCH / (PATCH - 1.0)
            )
            inv_std_of_group[g] = inv_std

        def normalise(g):
            r, parity = g // 2, (g + 1) % 2
            if g % 2 == 0:
                normed_of_round[r] = work.tile([P, 2 * PATCH], BF16, name="normed")
            patch = patch_of_group[g]
            inv_std = inv_std_of_group[g]
            nc.vector.tensor_scalar(
                out=normed_of_round[r][:, PATCH * parity : PATCH * (parity + 1)],
                in0=patch[:].bitcast(BF16)[:, 0:PATCH],
                scalar1=patch[:, GROUP_WORDS : GROUP_WORDS + 1],
                scalar2=inv_std[:],
                op0=ALU.add,
                op1=ALU.mult,
            )

        def channels_onto_partitions(r):
            normed_words = normed_of_round[r][:].bitcast(F32)
            back = psum_back.tile([P, BANK], F32, name="back")
            for slot in range(4):
                cols = slice(P * slot, P * (slot + 1))
                nc.tensor.transpose(back[:, cols], normed_words[:, cols], identity[:])
            back_of_round[r] = back

        def regroup(r):
            back = back_of_round[r]
            grouped = work.tile([P, ROUND_PIXELS * TAPS], BF16, name="grouped", align_bytes=64)
            nc.scalar.copy(
                out=grouped[:].bitcast(F32).rearrange("c (q s k) -> c q s k", s=2, k=2),
                in_=back[:].rearrange("c (s k q) -> c q s k", s=2, k=2),
            )
            grouped_of_round[r] = grouped

        def half_onto_partitions(r, slot):
            normed_words = normed_of_round[r][:, PATCH * (1 - slot) : PATCH * (2 - slot)].bitcast(F32)
            if r == 0 and slot == 0:
                back = psum_back.tile([P, BANK], F32, name="back")
            elif r == 0:
                back = psum_out.tile([P, BANK], F32, name="acc")
            else:
                back = psum_patch.tile([P, BANK], F32, name="patch")
            for kh in range(2):
                cols = slice(P * kh, P * (kh + 1))
                nc.tensor.transpose(back[:, cols], normed_words[:, cols], identity[:])
            back_of_round[r, slot] = back

        def regroup_half(r, slot, on_vector):
            grouped = work.tile([P, PATCH], BF16, name="grouped_half", align_bytes=64)
            ordered = grouped[:].bitcast(F32).rearrange("c (q k) -> c q k", k=2)
            words = back_of_round[r, slot][:, 0:GROUP_WORDS].rearrange("c (k q) -> c q k", k=2)
            if on_vector:
                nc.vector.tensor_copy(out=ordered, in_=words)
            else:
                nc.scalar.copy(out=ordered, in_=words)
            grouped_of_round[r, slot] = grouped

        def quantise_half(r, slot):
            x_codes = work.tile([P, P], U32, name="x_codes_half", align_bytes=64)
            x_scales = work.tile([P, P], U8, name="x_scales_half", align_bytes=64)
            nc.vector.quantize_mx(out=x_codes[:].bitcast(FP8X4), scales=x_scales[:], in_=grouped_of_round[r, slot][:])
            quantised_of_round[r, slot] = x_codes, x_scales

        def half_bank(r):
            if r == 0:
                bank = psum_out.tile([P, BANK], F32, name="acc")
            else:
                bank = psum_patch.tile([P, BANK], F32, name="patch")
            return bank

        def multiply_half(r, pair, slot):
            if slot == 0:
                products_of_round[r, pair] = half_bank(r)
            acc = products_of_round[r, pair]
            x_codes, x_scales = quantised_of_round[r, slot]
            for half in range(2):
                o_cols = slice(P * (2 * pair + half), P * (2 * pair + half + 1))
                nc.tensor.matmul_mx(
                    out=acc[:, ROUND_PIXELS * half + P * (1 - slot) : ROUND_PIXELS * half + P * (2 - slot)],
                    lhsT=w_codes[:, o_cols].bitcast(FP8X4),
                    lhsT_scale=w_scales[:, o_cols],
                    rhs=x_codes[:].bitcast(FP8X4),
                    rhs_scale=x_scales[:],
                    start=True,
                    stop=True,
                )

        def store_quarter(r, pair, half, on_vector):
            pixels = slice(ROUND_PIXELS * r, ROUND_PIXELS * (r + 1))
            result = results.tile([P, ROUND_PIXELS], F32, name="result_quarter")
            products = products_of_round[r, pair][:, ROUND_PIXELS * half : ROUND_PIXELS * (half + 1)]
            in_order = products.rearrange("p (s q) -> p q s", s=2)
            ordered = result[:].rearrange("p (q s) -> p q s", s=2)
            if on_vector:
                nc.vector.tensor_copy(out=ordered, in_=in_order)
            else:
                nc.scalar.copy(out=ordered, in_=in_order)
            nc.sync.dma_start(out=out_view[:, 2 * pair + half, pixels], in_=result[:])

        def quantise(r):
            x_codes = work.tile([P, ROUND_PIXELS], U32, name="x_codes", align_bytes=64)
            x_scales = work.tile([P, ROUND_PIXELS], U8, name="x_scales", align_bytes=64)
            nc.vector.quantize_mx(out=x_codes[:].bitcast(FP8X4), scales=x_scales[:], in_=grouped_of_round[r][:])
            quantised_of_round[r] = x_codes, x_scales

        def multiply(r, pair):
            x_codes, x_scales = quantised_of_round[r]
            acc = psum_out.tile([P, BANK], F32, name="acc")
            for half in range(2):
                o_cols = slice(P * (2 * pair + half), P * (2 * pair + half + 1))
                nc.tensor.matmul_mx(
                    out=acc[:, ROUND_PIXELS * half : ROUND_PIXELS * (half + 1)],
                    lhsT=w_codes[:, o_cols].bitcast(FP8X4),
                    lhsT_scale=w_scales[:, o_cols],
                    rhs=x_codes[:].bitcast(FP8X4),
                    rhs_scale=x_scales[:],
                    start=True,
                    stop=True,
                )
            products_of_round[r, pair] = acc

        def store(r, pair, on_vector=False):
            pixels = slice(ROUND_PIXELS * r, ROUND_PIXELS * (r + 1))
            result = results.tile([P, BANK], F32, name="result")
            if on_vector:
                nc.vector.tensor_copy(out=result[:], in_=products_of_round[r, pair][:])
            else:
                nc.scalar.copy(out=result[:], in_=products_of_round[r, pair][:])
            nc.sync.dma_start(out=out_view[:, 2 * pair : 2 * pair + 2, pixels], in_=result[:].rearrange("p (t x) -> p t x", t=2))

        def quantise_weights(half):
            nc.vector.quantize_mx(
                out=w_codes[:, half].bitcast(FP8X4),
                scales=w_scales[:, half],
                in_=w_grouped[:, half, :].rearrange("c o t -> c (o t)"),
            )

        pixels_onto_partitions(0)
        keep_warm(1)
        shift(nc.vector.tensor_copy, 0, TOP_ROWS)
        measure(0)
        shift(nc.scalar.copy, TOP_ROWS, SIDE + 1)
        pixels_onto_partitions(1)
        pixels_onto_partitions(2)
        keep_warm(1)
        sum_patches(1)
        sum_patches(0)
        spread(0)
        root(0)
        fetch_mean(1)
        square(1)
        measure(2)
        pixels_onto_partitions(3)
        pixels_onto_partitions(4)
        keep_warm(1)
        sum_patches(3)
        normalise(0)
        half_onto_partitions(0, 0)
        keep_warm(1)
        spread(2)
        root(2)
        root_of_square(1)
        measure(4)
        fetch_mean(3)
        square(3)
        sum_patches(2)
        pixels_onto_partitions(5)
        normalise(1)
        half_onto_partitions(0, 1)
        keep_warm(1)
        spread(4)
        root_of_square(3)
        regroup_half(0, 0, False)
        root(4)
        sum_patches(4)
        normalise(2)
        measure(5)
        pixels_onto_partitions(6)
        normalise(3)
        regroup_half(0, 1, False)
        channels_onto_partitions(1)
        sum_patches(5)
        quantise_half(0, 0)
        spread(5)
        root(5)
        quantise_weights(W_HALVES[0])
        quantise_half(0, 1)
        multiply_half(0, 0, 0)
        multiply_half(0, 0, 1)
        quantise_weights(W_HALVES[1])
        multiply_half(0, 1, 0)
        multiply_half(0, 1, 1)
        pixels_onto_partitions(7)
        regroup(1)
        store_quarter(0, 0, 0, False)
        store_quarter(0, 0, 1, False)
        store_quarter(0, 1, 0, False)
        store_quarter(0, 1, 1, False)
        normalise(4)
        normalise(5)
        channels_onto_partitions(2)
        measure(6)
        quantise(1)
        multiply(1, 0)
        multiply(1, 1)
        sum_patches(6)
        regroup(2)
        measure(7)
        sum_patches(7)
        spread(6)
        root(6)
        spread(7)
        root(7)
        store(1, 0)
        store(1, 1)
        quantise(2)
        multiply(2, 0)
        normalise(6)
        half_onto_partitions(3, 0)
        normalise(7)
        half_onto_partitions(3, 1)
        multiply(2, 1)
        regroup_half(3, 0, False)
        regroup_half(3, 1, False)
        store(2, 0, True)
        quantise_half(3, 0)
        quantise_half(3, 1)
        store(2, 1)
        for slot in range(2):
            for pair in range(2):
                multiply_half(3, pair, slot)
        for half in range(2):
            store_quarter(3, 0, half, False)
            store_quarter(3, 1, half, True)
